import numpy as np
import ml_dtypes


def mxq(x, axis, fmt="e4m3"):
    dtype, down = {"e4m3": (ml_dtypes.float8_e4m3fn, 7), "e5m2": (ml_dtypes.float8_e5m2, 14)}[fmt]
    v = np.moveaxis(np.asarray(x, np.float32).astype(ml_dtypes.bfloat16).astype(np.float64), axis, -1)
    blocks = v.reshape(v.shape[:-1] + (-1, 32))
    amax = np.abs(blocks).max(-1, keepdims=True)
    byte = np.maximum(np.where(amax > 0, np.frexp(amax)[1] - 1 + 127, 0) - down, 1)
    scale = np.exp2(byte - 127.0)
    codes = (blocks / scale).astype(np.float32).astype(dtype).astype(np.float64)
    return np.moveaxis((codes * scale).reshape(v.shape), -1, axis)


BF16 = ml_dtypes.bfloat16


def bf(x):
    return np.asarray(x, np.float32).astype(BF16)


def f64(x):
    return np.asarray(x).astype(np.float64)


B, D, HH, WW = 16, 512, 16, 32
M = HH * WW


def setup_inputs():
    n = np.random.standard_normal((B, D, HH, WW))
    g = np.random.standard_normal((B, HH, WW))[:, None]
    a = np.random.standard_normal((B, D))[:, :, None, None]
    mu = np.random.standard_normal((B, D))[:, :, None, None]
    return {"x": bf(n + a * g + mu)}


def reference(x):
    xf = f64(x).reshape(B, D, M)
    inv_m = 1.0 / M
    xi = inv_m * xf - (inv_m * inv_m) * xf.sum(-1, keepdims=True)
    return mxq(xi, 2, "e4m3") @ mxq(xf, 2, "e4m3").transpose(0, 2, 1)

@@ -1,0 +1,137 @@
+from contextlib import ExitStack
+
+import concourse.masks as masks
+import concourse.mybir as mybir
+
+BF16 = mybir.dt.bfloat16
+F32 = mybir.dt.float32
+U32 = mybir.dt.uint32
+U8 = mybir.dt.uint8
+FP8X4 = mybir.dt.float8_e4m3fn_x4
+ALU = mybir.AluOpType
+ACT = mybir.ActivationFunctionType
+
+P = 128
+B = 16
+D = 512
+M = 512
+C = D // P
+FLOPS = 2 * B * D * D * M
+
+INV_M = 1.0 / M
+INV_M2 = INV_M * INV_M
+
+SUM_ON_SCALAR = (3,)
+
+
+def tile_covpool_pa_kernel(tc, x, out):
+    nc = tc.nc
+    x_rows = x.rearrange("b (p c) h w -> b p (c h w)", c=C)
+    out_rows = out.rearrange("b (p c) j -> b p (c j)", c=C)
+
+    with ExitStack() as ctx:
+        const = ctx.enter_context(tc.tile_pool(name="const", bufs=1))
+        xin = ctx.enter_context(tc.tile_pool(name="xin", bufs=1))
+        grp = ctx.enter_context(tc.tile_pool(name="grp", bufs=4))
+        cod = ctx.enter_context(tc.tile_pool(name="cod", bufs=3))
+        small = ctx.enter_context(tc.tile_pool(name="small", bufs=4))
+        junk = ctx.enter_context(tc.tile_pool(name="junk", bufs=2))
+        ysb = ctx.enter_context(tc.tile_pool(name="ysb", bufs=3))
+        ps_xt = ctx.enter_context(tc.psum_pool(name="ps_xt", bufs=2))
+        ps_sb = ctx.enter_context(tc.psum_pool(name="ps_sb", bufs=2))
+        ps_y = ctx.enter_context(tc.psum_pool(name="ps_y", bufs=4))
+
+        ident = const.tile([P, P], F32, name="ident")
+        masks.make_identity(nc, ident[:])
+
+        x_sb = []
+        for b in range(B):
+            t = xin.tile([P, C * M], BF16, name="x%d" % b)
+            nc.sync.dma_start(out=t[:], in_=x_rows[b])
+            x_sb.append(t)
+
+        st = {}
+
+        def stage_a(b):
+            xw = x_sb[b][:].bitcast(F32)
+            x_g = grp.tile([P, D * 4], BF16, name="x_g", align_bytes=64)
+            x_gw = x_g[:].bitcast(F32).rearrange("p (r k) -> p r k", k=8)
+            for h in range(2):
+                xt = ps_xt.tile([P, 4, P], F32, name="xt")
+                for k in range(4):
+                    col = (4 * h + k) * P
+                    nc.tensor.transpose(xt[:, k, :], xw[:, col : col + P], ident[:])
+                nc.scalar.copy(
+                    out=x_gw[:, :, 4 * h : 4 * h + 4],
+                    in_=xt[:].rearrange("p k r -> p r k"),
+                )
+            smv = small.tile([P, C], F32, name="smv")
+            sms = small.tile([P, C], F32, name="sms")
+            for c in range(C):
+                src = x_sb[b][:, c * M : (c + 1) * M]
+                if c in SUM_ON_SCALAR:
+                    js = junk.tile([P, M], BF16, name="js")
+                    nc.scalar.activation(
+                        out=js[:], in_=src, func=ACT.Copy, scale=INV_M2,
+                        accum_out=sms[:, c : c + 1],
+                    )
+                else:
+                    jv = junk.tile([P, M], BF16, name="jv")
+                    nc.vector.tensor_scalar(
+                        out=jv[:], in0=src, scalar1=INV_M2, scalar2=None,
+                        op0=ALU.mult, op1=ALU.add, accum_out=smv[:, c : c + 1],
+                    )
+            st[b] = {"x_g": x_g, "smv": smv, "sms": sms}
+
+        def stage_b(b):
+            s = st[b]
+            x_g = s["x_g"]
+            sbp = ps_sb.tile([P, C, P], F32, name="sbp")
+            for c in range(C):
+                sm = s["sms"] if c in SUM_ON_SCALAR else s["smv"]
+                nc.tensor.transpose(
+                    sbp[:, c, :], sm[:, c : c + 1].to_broadcast([P, P]), ident[:]
+                )
+            xc = cod.tile([P, D], U32, name="xc", align_bytes=64)
+            xs = cod.tile([P, D], U8, name="xs", align_bytes=64)
+            nc.vector.quantize_mx(out=xc[:].bitcast(FP8X4), scales=xs[:], in_=x_g[:])
+            xi_g = grp.tile([P, D * 4], BF16, name="xi_g", align_bytes=64)
+            x_v = x_g[:].rearrange("p (r c t) -> p r c t", c=C, t=4)
+            for c in range(C):
+                nc.vector.scalar_tensor_tensor(
+                    out=xi_g[:, c * 512 : (c + 1) * 512].rearrange("p (r t) -> p r t", t=4),
+                    in0=x_v[:, :, c, :],
+                    scalar=INV_M,
+                    in1=sbp[:, c, :].unsqueeze(2).to_broadcast([P, P, 4]),
+                    op0=ALU.mult,
+                    op1=ALU.subtract,
+                )
+            xic = cod.tile([P, D], U32, name="xic", align_bytes=64)
+            xis = cod.tile([P, D], U8, name="xis", align_bytes=64)
+            nc.vector.quantize_mx(out=xic[:].bitcast(FP8X4), scales=xis[:], in_=xi_g[:])
+            s["codes"] = (xc, xs, xic, xis)
+
+        def stage_c(b):
+            xc, xs, xic, xis = st[b]["codes"]
+            y_sb = ysb.tile([P, C * D], F32, name="y_sb")
+            for c in range(C):
+                y_ps = ps_y.tile([P, D], F32, name="y_ps")
+                nc.tensor.matmul_mx(
+                    out=y_ps[:],
+                    lhsT=xic[:, c * P : (c + 1) * P].bitcast(FP8X4),
+                    lhsT_scale=xis[:, c * P : (c + 1) * P],
+                    rhs=xc[:].bitcast(FP8X4),
+                    rhs_scale=xs[:],
+                    start=True,
+                    stop=True,
+                )
+                nc.scalar.copy(out=y_sb[:, c * D : (c + 1) * D], in_=y_ps[:])
+            nc.sync.dma_start(out=out_rows[b], in_=y_sb[:])
+
+        for i in range(B + 2):
+            if i < B:
+                stage_a(i)
+            if 0 <= i - 1 < B:
+                stage_b(i - 1)
+            if 0 <= i - 2 < B:
+                stage_c(i - 2)

@@ -21,7 +21,15 @@ FLOPS = 2 * B * D * D * M
 INV_M = 1.0 / M
 INV_M2 = INV_M * INV_M
 
-SUM_ON_SCALAR = (3,)
+PIN = True
+
+
+def sums_on_scalar(b):
+    return (3,) if b % 2 == 0 else (2, 3)
+
+
+def y_on_vector(b):
+    return (1, 3) if b == B - 1 else ()
 
 
 def tile_covpool_pa_kernel(tc, x, out):
@@ -33,6 +41,7 @@ def tile_covpool_pa_kernel(tc, x, out):
         const = ctx.enter_context(tc.tile_pool(name="const", bufs=1))
         xin = ctx.enter_context(tc.tile_pool(name="xin", bufs=1))
         grp = ctx.enter_context(tc.tile_pool(name="grp", bufs=4))
+        grp2 = ctx.enter_context(tc.tile_pool(name="grp2", bufs=2))
         cod = ctx.enter_context(tc.tile_pool(name="cod", bufs=3))
         small = ctx.enter_context(tc.tile_pool(name="small", bufs=4))
         junk = ctx.enter_context(tc.tile_pool(name="junk", bufs=2))
@@ -40,6 +49,8 @@ def tile_covpool_pa_kernel(tc, x, out):
         ps_xt = ctx.enter_context(tc.psum_pool(name="ps_xt", bufs=2))
         ps_sb = ctx.enter_context(tc.psum_pool(name="ps_sb", bufs=2))
         ps_y = ctx.enter_context(tc.psum_pool(name="ps_y", bufs=4))
+        if PIN:
+            ctx.enter_context(tc.manual_schedule())
 
         ident = const.tile([P, P], F32, name="ident")
         masks.make_identity(nc, ident[:])
@@ -47,29 +58,39 @@ def tile_covpool_pa_kernel(tc, x, out):
         x_sb = []
         for b in range(B):
             t = xin.tile([P, C * M], BF16, name="x%d" % b)
-            nc.sync.dma_start(out=t[:], in_=x_rows[b])
+            if b == 0:
+                half = C * M // 2
+                nc.sync.dma_start(out=t[:, 0:half], in_=x_rows[b][:, 0:half])
+                nc.sync.dma_start(out=t[:, half:], in_=x_rows[b][:, half:])
+            else:
+                nc.sync.dma_start(out=t[:], in_=x_rows[b])
             x_sb.append(t)
 
         st = {}
 
-        def stage_a(b):
+        def transposes(b):
             xw = x_sb[b][:].bitcast(F32)
             x_g = grp.tile([P, D * 4], BF16, name="x_g", align_bytes=64)
-            x_gw = x_g[:].bitcast(F32).rearrange("p (r k) -> p r k", k=8)
+            x_gw = x_g[:].bitcast(F32)
             for h in range(2):
                 xt = ps_xt.tile([P, 4, P], F32, name="xt")
                 for k in range(4):
                     col = (4 * h + k) * P
                     nc.tensor.transpose(xt[:, k, :], xw[:, col : col + P], ident[:])
                 nc.scalar.copy(
-                    out=x_gw[:, :, 4 * h : 4 * h + 4],
-                    in_=xt[:].rearrange("p k r -> p r k"),
+                    out=x_gw[:, h * 512 : (h + 1) * 512].rearrange(
+                        "p (c r u) -> p c r u", c=2, u=2
+                    ),
+                    in_=xt[:].rearrange("p (c u) r -> p c r u", c=2),
                 )
+            st[b] = {"x_g": x_g}
+
+        def sums(b):
             smv = small.tile([P, C], F32, name="smv")
             sms = small.tile([P, C], F32, name="sms")
             for c in range(C):
                 src = x_sb[b][:, c * M : (c + 1) * M]
-                if c in SUM_ON_SCALAR:
+                if c in sums_on_scalar(b):
                     js = junk.tile([P, M], BF16, name="js")
                     nc.scalar.activation(
                         out=js[:], in_=src, func=ACT.Copy, scale=INV_M2,
@@ -81,57 +102,81 @@ def tile_covpool_pa_kernel(tc, x, out):
                         out=jv[:], in0=src, scalar1=INV_M2, scalar2=None,
                         op0=ALU.mult, op1=ALU.add, accum_out=smv[:, c : c + 1],
                     )
-            st[b] = {"x_g": x_g, "smv": smv, "sms": sms}
+            st[b]["smv"] = smv
+            st[b]["sms"] = sms
 
-        def stage_b(b):
+        def spread_sums(b):
             s = st[b]
-            x_g = s["x_g"]
             sbp = ps_sb.tile([P, C, P], F32, name="sbp")
             for c in range(C):
-                sm = s["sms"] if c in SUM_ON_SCALAR else s["smv"]
+                sm = s["sms"] if c in sums_on_scalar(b) else s["smv"]
                 nc.tensor.transpose(
                     sbp[:, c, :], sm[:, c : c + 1].to_broadcast([P, P]), ident[:]
                 )
-            xc = cod.tile([P, D], U32, name="xc", align_bytes=64)
-            xs = cod.tile([P, D], U8, name="xs", align_bytes=64)
-            nc.vector.quantize_mx(out=xc[:].bitcast(FP8X4), scales=xs[:], in_=x_g[:])
-            xi_g = grp.tile([P, D * 4], BF16, name="xi_g", align_bytes=64)
-            x_v = x_g[:].rearrange("p (r c t) -> p r c t", c=C, t=4)
-            for c in range(C):
-                nc.vector.scalar_tensor_tensor(
-                    out=xi_g[:, c * 512 : (c + 1) * 512].rearrange("p (r t) -> p r t", t=4),
-                    in0=x_v[:, :, c, :],
-                    scalar=INV_M,
-                    in1=sbp[:, c, :].unsqueeze(2).to_broadcast([P, P, 4]),
-                    op0=ALU.mult,
-                    op1=ALU.subtract,
-                )
-            xic = cod.tile([P, D], U32, name="xic", align_bytes=64)
-            xis = cod.tile([P, D], U8, name="xis", align_bytes=64)
-            nc.vector.quantize_mx(out=xic[:].bitcast(FP8X4), scales=xis[:], in_=xi_g[:])
-            s["codes"] = (xc, xs, xic, xis)
+            s["sbp"] = sbp
 
-        def stage_c(b):
-            xc, xs, xic, xis = st[b]["codes"]
+        def centre(b):
+            s = st[b]
+            xi_g = grp2.tile([P, D * 4], BF16, name="xi_g", align_bytes=64)
+            nc.vector.scalar_tensor_tensor(
+                out=xi_g[:].rearrange("p (n t) -> p n t", t=4),
+                in0=s["x_g"][:].rearrange("p (n t) -> p n t", t=4),
+                scalar=INV_M,
+                in1=s["sbp"][:].rearrange("p c r -> p (c r)").unsqueeze(2).to_broadcast([P, D, 4]),
+                op0=ALU.mult,
+                op1=ALU.subtract,
+            )
+            s["xi_g"] = xi_g
+
+        def quantise(b, key, cname, sname):
+            codes = cod.tile([P, D], U32, name=cname, align_bytes=64)
+            scales = cod.tile([P, D], U8, name=sname, align_bytes=64)
+            nc.vector.quantize_mx(
+                out=codes[:].bitcast(FP8X4), scales=scales[:], in_=st[b][key][:]
+            )
+            st[b][cname] = codes
+            st[b][sname] = scales
+
+        def multiply(b):
+            s = st[b]
             y_sb = ysb.tile([P, C * D], F32, name="y_sb")
+            last = b == B - 1
             for c in range(C):
                 y_ps = ps_y.tile([P, D], F32, name="y_ps")
                 nc.tensor.matmul_mx(
                     out=y_ps[:],
-                    lhsT=xic[:, c * P : (c + 1) * P].bitcast(FP8X4),
-                    lhsT_scale=xis[:, c * P : (c + 1) * P],
-                    rhs=xc[:].bitcast(FP8X4),
-                    rhs_scale=xs[:],
+                    lhsT=s["xic"][:, c * P : (c + 1) * P].bitcast(FP8X4),
+                    lhsT_scale=s["xis"][:, c * P : (c + 1) * P],
+                    rhs=s["xc"][:].bitcast(FP8X4),
+                    rhs_scale=s["xs"][:],
                     start=True,
                     stop=True,
                 )
-                nc.scalar.copy(out=y_sb[:, c * D : (c + 1) * D], in_=y_ps[:])
-            nc.sync.dma_start(out=out_rows[b], in_=y_sb[:])
+                dst = y_sb[:, c * D : (c + 1) * D].rearrange("p (r c) -> p r c", c=C)
+                src = y_ps[:].rearrange("p (c r) -> p r c", c=C)
+                if c in y_on_vector(b):
+                    nc.vector.tensor_copy(out=dst, in_=src)
+                else:
+                    nc.scalar.copy(out=dst, in_=src)
+                if last:
+                    nc.sync.dma_start(
+                        out=out_rows[b][:, c * D : (c + 1) * D],
+                        in_=y_sb[:, c * D : (c + 1) * D],
+                    )
+            if not last:
+                nc.sync.dma_start(out=out_rows[b], in_=y_sb[:])
 
-        for i in range(B + 2):
-            if i < B:
-                stage_a(i)
-            if 0 <= i - 1 < B:
-                stage_b(i - 1)
-            if 0 <= i - 2 < B:
-                stage_c(i - 2)
+        for j in range(-2, B + 1):
+            if j + 2 < B:
+                transposes(j + 2)
+            if 0 <= j + 1 < B:
+                spread_sums(j + 1)
+            if 0 <= j < B:
+                centre(j)
+                quantise(j, "x_g", "xc", "xs")
+            if j + 2 < B:
+                sums(j + 2)
+            if 0 <= j < B:
+                quantise(j, "xi_g", "xic", "xis")
+            if 0 <= j - 1 < B:
+                multiply(j - 1)

@@ -21,11 +21,13 @@ FLOPS = 2 * B * D * D * M
 INV_M = 1.0 / M
 INV_M2 = INV_M * INV_M
 
+G_CHUNKS = 3
+G_FROM = 2
 PIN = True
 
 
 def sums_on_scalar(b):
-    return (3,) if b % 2 == 0 else (2, 3)
+    return (3,) if b >= G_FROM or b % 2 == 0 else (2, 3)
 
 
 def y_on_vector(b):
@@ -44,6 +46,8 @@ def tile_covpool_pa_kernel(tc, x, out):
         grp2 = ctx.enter_context(tc.tile_pool(name="grp2", bufs=2))
         cod = ctx.enter_context(tc.tile_pool(name="cod", bufs=3))
         small = ctx.enter_context(tc.tile_pool(name="small", bufs=4))
+        gp1 = ctx.enter_context(tc.tile_pool(name="gp1", bufs=2))
+        gp2 = ctx.enter_context(tc.tile_pool(name="gp2", bufs=3))
         junk = ctx.enter_context(tc.tile_pool(name="junk", bufs=2))
         ysb = ctx.enter_context(tc.tile_pool(name="ysb", bufs=3))
         ps_xt = ctx.enter_context(tc.psum_pool(name="ps_xt", bufs=2))
@@ -67,6 +71,7 @@ def tile_covpool_pa_kernel(tc, x, out):
             x_sb.append(t)
 
         st = {}
+        gs = {}
 
         def transposes(b):
             xw = x_sb[b][:].bitcast(F32)
@@ -85,10 +90,34 @@ def tile_covpool_pa_kernel(tc, x, out):
                 )
             st[b] = {"x_g": x_g}
 
-        def sums(b):
+        def pool_sums(b):
+            if b < G_FROM:
+                return
+            xv = x_sb[b][:, 0 : G_CHUNKS * M].rearrange("p (c m) -> p c m", c=G_CHUNKS)
+            g1 = gp1.tile([P, G_CHUNKS, M // 2], F32, name="g1")
+            nc.gpsimd.tensor_tensor(
+                out=g1[:], in0=xv[:, :, 0 : M // 2], in1=xv[:, :, M // 2 : M], op=ALU.add
+            )
+            g2 = gp2.tile([P, G_CHUNKS, M // 4], F32, name="g2")
+            nc.gpsimd.tensor_tensor(
+                out=g2[:], in0=g1[:, :, 0 : M // 4], in1=g1[:, :, M // 4 : M // 2], op=ALU.add
+            )
+            gs[b] = g2
+
+        def sums_a(b):
             smv = small.tile([P, C], F32, name="smv")
             sms = small.tile([P, C], F32, name="sms")
+            st[b]["smv"] = smv
+            st[b]["sms"] = sms
+            if b >= G_FROM:
+                raw = small.tile([P, C], F32, name="raw")
+                nc.vector.tensor_reduce(
+                    out=raw[:, 0:G_CHUNKS], in_=gs[b][:], axis=mybir.AxisListType.X, op=ALU.add
+                )
+                st[b]["raw"] = raw
             for c in range(C):
+                if b >= G_FROM and c < G_CHUNKS:
+                    continue
                 src = x_sb[b][:, c * M : (c + 1) * M]
                 if c in sums_on_scalar(b):
                     js = junk.tile([P, M], BF16, name="js")
@@ -102,8 +131,13 @@ def tile_covpool_pa_kernel(tc, x, out):
                         out=jv[:], in0=src, scalar1=INV_M2, scalar2=None,
                         op0=ALU.mult, op1=ALU.add, accum_out=smv[:, c : c + 1],
                     )
-            st[b]["smv"] = smv
-            st[b]["sms"] = sms
+
+        def sums_b(b):
+            if b >= G_FROM:
+                nc.vector.tensor_scalar(
+                    out=st[b]["smv"][:, 0:G_CHUNKS], in0=st[b]["raw"][:, 0:G_CHUNKS],
+                    scalar1=INV_M2, scalar2=None, op0=ALU.mult,
+                )
 
         def spread_sums(b):
             s = st[b]
@@ -167,15 +201,23 @@ def tile_covpool_pa_kernel(tc, x, out):
                 nc.sync.dma_start(out=out_rows[b], in_=y_sb[:])
 
         for j in range(-2, B + 1):
+            if 0 <= j + 3 < B:
+                pool_sums(j + 3)
+            if j == -2:
+                for b in range(3 - 2):
+                    pool_sums(b)
             if j + 2 < B:
                 transposes(j + 2)
             if 0 <= j + 1 < B:
                 spread_sums(j + 1)
             if 0 <= j < B:
                 centre(j)
+            if j + 2 < B:
+                sums_a(j + 2)
+            if 0 <= j < B:
                 quantise(j, "x_g", "xc", "xs")
             if j + 2 < B:
-                sums(j + 2)
+                sums_b(j + 2)
             if 0 <= j < B:
                 quantise(j, "xi_g", "xic", "xis")
             if 0 <= j - 1 < B:

@@ -9,7 +9,6 @@ U32 = mybir.dt.uint32
 U8 = mybir.dt.uint8
 FP8X4 = mybir.dt.float8_e4m3fn_x4
 ALU = mybir.AluOpType
-ACT = mybir.ActivationFunctionType
 
 P = 128
 B = 16
@@ -19,19 +18,14 @@ C = D // P
 FLOPS = 2 * B * D * D * M
 
 INV_M = 1.0 / M
-INV_M2 = INV_M * INV_M
-
-G_CHUNKS = 3
-G_FROM = 2
-PIN = True
 
 
-def sums_on_scalar(b):
-    return (3,) if b >= G_FROM or b % 2 == 0 else (2, 3)
+def x_on_vector(b, h):
+    return b < 2 and h == 1
 
 
-def y_on_vector(b):
-    return (1, 3) if b == B - 1 else ()
+def y_on_vector(b, c):
+    return c == 3 and (b % 2 == 1) or (b == B - 1 and c == 1)
 
 
 def tile_covpool_pa_kernel(tc, x, out):
@@ -42,183 +36,164 @@ def tile_covpool_pa_kernel(tc, x, out):
     with ExitStack() as ctx:
         const = ctx.enter_context(tc.tile_pool(name="const", bufs=1))
         xin = ctx.enter_context(tc.tile_pool(name="xin", bufs=1))
-        grp = ctx.enter_context(tc.tile_pool(name="grp", bufs=4))
-        grp2 = ctx.enter_context(tc.tile_pool(name="grp2", bufs=2))
+        grp = ctx.enter_context(tc.tile_pool(name="grp", bufs=3))
         cod = ctx.enter_context(tc.tile_pool(name="cod", bufs=3))
         small = ctx.enter_context(tc.tile_pool(name="small", bufs=4))
-        gp1 = ctx.enter_context(tc.tile_pool(name="gp1", bufs=2))
-        gp2 = ctx.enter_context(tc.tile_pool(name="gp2", bufs=3))
-        junk = ctx.enter_context(tc.tile_pool(name="junk", bufs=2))
-        ysb = ctx.enter_context(tc.tile_pool(name="ysb", bufs=3))
-        ps_xt = ctx.enter_context(tc.psum_pool(name="ps_xt", bufs=2))
-        ps_sb = ctx.enter_context(tc.psum_pool(name="ps_sb", bufs=2))
-        ps_y = ctx.enter_context(tc.psum_pool(name="ps_y", bufs=4))
-        if PIN:
-            ctx.enter_context(tc.manual_schedule())
+        ysb = ctx.enter_context(tc.tile_pool(name="ysb", bufs=4))
+        ps_t = ctx.enter_context(tc.psum_pool(name="ps_t", bufs=4))
+        ps_s = ctx.enter_context(tc.psum_pool(name="ps_s", bufs=1))
+        ps_y = ctx.enter_context(tc.psum_pool(name="ps_y", bufs=3))
+        ctx.enter_context(tc.manual_schedule())
 
         ident = const.tile([P, P], F32, name="ident")
         masks.make_identity(nc, ident[:])
+        inv_m = const.tile([P, 2], BF16, name="inv_m")
+        nc.vector.memset(inv_m[:], INV_M)
 
         x_sb = []
         for b in range(B):
             t = xin.tile([P, C * M], BF16, name="x%d" % b)
-            if b == 0:
-                half = C * M // 2
-                nc.sync.dma_start(out=t[:, 0:half], in_=x_rows[b][:, 0:half])
-                nc.sync.dma_start(out=t[:, half:], in_=x_rows[b][:, half:])
-            else:
-                nc.sync.dma_start(out=t[:], in_=x_rows[b])
+            pieces = C if b == 0 else 1
+            w = C * M // pieces
+            for i in range(pieces):
+                nc.sync.dma_start(out=t[:, i * w : (i + 1) * w], in_=x_rows[b][:, i * w : (i + 1) * w])
             x_sb.append(t)
 
-        st = {}
-        gs = {}
+        st = [{} for _ in range(B)]
 
-        def transposes(b):
-            xw = x_sb[b][:].bitcast(F32)
+        def copy(on_vector, dst, src):
+            if on_vector:
+                nc.vector.tensor_copy(out=dst, in_=src)
+            else:
+                nc.scalar.copy(out=dst, in_=src)
+
+        def transpose_half(b, src, h):
+            tp = ps_t.tile([P, 4, P], F32, name="tp")
+            sw = src[:].bitcast(F32)
+            for k in range(4):
+                col = (4 * h + k) * P
+                nc.tensor.transpose(tp[:, k, :], sw[:, col : col + P], ident[:])
+            return tp
+
+        def group_half(on_vector, dst, tp, h):
+            copy(
+                on_vector,
+                dst[:].bitcast(F32)[:, h * 512 : (h + 1) * 512].rearrange("p (c r u) -> p c r u", c=2, u=2),
+                tp[:].rearrange("p (c u) r -> p c r u", c=2),
+            )
+
+        def quantise(b, src, name):
+            codes = cod.tile([P, D], U32, name=name + "c", align_bytes=64)
+            scales = cod.tile([P, D], U8, name=name + "s", align_bytes=64)
+            nc.vector.quantize_mx(out=codes[:].bitcast(FP8X4), scales=scales[:], in_=src[:])
+            st[b][name] = (codes, scales)
+
+        def ta(b):
+            st[b]["tx"] = [transpose_half(b, x_sb[b], h) for h in range(2)]
+
+        def bx(b):
             x_g = grp.tile([P, D * 4], BF16, name="x_g", align_bytes=64)
-            x_gw = x_g[:].bitcast(F32)
+            st[b]["x_g"] = x_g
             for h in range(2):
-                xt = ps_xt.tile([P, 4, P], F32, name="xt")
-                for k in range(4):
-                    col = (4 * h + k) * P
-                    nc.tensor.transpose(xt[:, k, :], xw[:, col : col + P], ident[:])
-                nc.scalar.copy(
-                    out=x_gw[:, h * 512 : (h + 1) * 512].rearrange(
-                        "p (c r u) -> p c r u", c=2, u=2
-                    ),
-                    in_=xt[:].rearrange("p (c u) r -> p c r u", c=2),
-                )
-            st[b] = {"x_g": x_g}
+                group_half(x_on_vector(b, h), x_g, st[b]["tx"][h], h)
 
-        def pool_sums(b):
-            if b < G_FROM:
-                return
-            xv = x_sb[b][:, 0 : G_CHUNKS * M].rearrange("p (c m) -> p c m", c=G_CHUNKS)
-            g1 = gp1.tile([P, G_CHUNKS, M // 2], F32, name="g1")
-            nc.gpsimd.tensor_tensor(
-                out=g1[:], in0=xv[:, :, 0 : M // 2], in1=xv[:, :, M // 2 : M], op=ALU.add
-            )
-            g2 = gp2.tile([P, G_CHUNKS, M // 4], F32, name="g2")
-            nc.gpsimd.tensor_tensor(
-                out=g2[:], in0=g1[:, :, 0 : M // 4], in1=g1[:, :, M // 4 : M // 2], op=ALU.add
-            )
-            gs[b] = g2
-
-        def sums_a(b):
-            smv = small.tile([P, C], F32, name="smv")
-            sms = small.tile([P, C], F32, name="sms")
-            st[b]["smv"] = smv
-            st[b]["sms"] = sms
-            if b >= G_FROM:
-                raw = small.tile([P, C], F32, name="raw")
-                nc.vector.tensor_reduce(
-                    out=raw[:, 0:G_CHUNKS], in_=gs[b][:], axis=mybir.AxisListType.X, op=ALU.add
-                )
-                st[b]["raw"] = raw
+        def means(b):
+            ms = ps_s.tile([P, C], F32, name="ms")
+            xv = st[b]["x_g"][:].rearrange("p (n t) -> p n t", t=4)
             for c in range(C):
-                if b >= G_FROM and c < G_CHUNKS:
-                    continue
-                src = x_sb[b][:, c * M : (c + 1) * M]
-                if c in sums_on_scalar(b):
-                    js = junk.tile([P, M], BF16, name="js")
-                    nc.scalar.activation(
-                        out=js[:], in_=src, func=ACT.Copy, scale=INV_M2,
-                        accum_out=sms[:, c : c + 1],
+                for t in range(4):
+                    nc.tensor.matmul(
+                        ms[:, c : c + 1],
+                        lhsT=xv[:, c * P : (c + 1) * P, t],
+                        rhs=inv_m[:, 0:1],
+                        start=(t == 0),
+                        stop=(t == 3),
                     )
-                else:
-                    jv = junk.tile([P, M], BF16, name="jv")
-                    nc.vector.tensor_scalar(
-                        out=jv[:], in0=src, scalar1=INV_M2, scalar2=None,
-                        op0=ALU.mult, op1=ALU.add, accum_out=smv[:, c : c + 1],
-                    )
+            st[b]["ms"] = ms
 
-        def sums_b(b):
-            if b >= G_FROM:
-                nc.vector.tensor_scalar(
-                    out=st[b]["smv"][:, 0:G_CHUNKS], in0=st[b]["raw"][:, 0:G_CHUNKS],
-                    scalar1=INV_M2, scalar2=None, op0=ALU.mult,
-                )
-
-        def spread_sums(b):
-            s = st[b]
-            sbp = ps_sb.tile([P, C, P], F32, name="sbp")
-            for c in range(C):
-                sm = s["sms"] if c in sums_on_scalar(b) else s["smv"]
-                nc.tensor.transpose(
-                    sbp[:, c, :], sm[:, c : c + 1].to_broadcast([P, P]), ident[:]
-                )
-            s["sbp"] = sbp
+        def mean_copy(b):
+            mean = small.tile([P, C], F32, name="mean")
+            nc.scalar.copy(out=mean[:], in_=st[b]["ms"][:])
+            st[b]["mean"] = mean
 
         def centre(b):
-            s = st[b]
-            xi_g = grp2.tile([P, D * 4], BF16, name="xi_g", align_bytes=64)
-            nc.vector.scalar_tensor_tensor(
-                out=xi_g[:].rearrange("p (n t) -> p n t", t=4),
-                in0=s["x_g"][:].rearrange("p (n t) -> p n t", t=4),
-                scalar=INV_M,
-                in1=s["sbp"][:].rearrange("p c r -> p (c r)").unsqueeze(2).to_broadcast([P, D, 4]),
-                op0=ALU.mult,
-                op1=ALU.subtract,
-            )
-            s["xi_g"] = xi_g
-
-        def quantise(b, key, cname, sname):
-            codes = cod.tile([P, D], U32, name=cname, align_bytes=64)
-            scales = cod.tile([P, D], U8, name=sname, align_bytes=64)
-            nc.vector.quantize_mx(
-                out=codes[:].bitcast(FP8X4), scales=scales[:], in_=st[b][key][:]
-            )
-            st[b][cname] = codes
-            st[b][sname] = scales
-
-        def multiply(b):
-            s = st[b]
-            y_sb = ysb.tile([P, C * D], F32, name="y_sb")
-            last = b == B - 1
+            xi = grp.tile([P, C * M], BF16, name="xi")
             for c in range(C):
-                y_ps = ps_y.tile([P, D], F32, name="y_ps")
-                nc.tensor.matmul_mx(
-                    out=y_ps[:],
-                    lhsT=s["xic"][:, c * P : (c + 1) * P].bitcast(FP8X4),
-                    lhsT_scale=s["xis"][:, c * P : (c + 1) * P],
-                    rhs=s["xc"][:].bitcast(FP8X4),
-                    rhs_scale=s["xs"][:],
-                    start=True,
-                    stop=True,
+                nc.vector.tensor_scalar(
+                    out=xi[:, c * M : (c + 1) * M],
+                    in0=x_sb[b][:, c * M : (c + 1) * M],
+                    scalar1=st[b]["mean"][:, c : c + 1],
+                    scalar2=INV_M,
+                    op0=ALU.subtract,
+                    op1=ALU.mult,
                 )
-                dst = y_sb[:, c * D : (c + 1) * D].rearrange("p (r c) -> p r c", c=C)
-                src = y_ps[:].rearrange("p (c r) -> p r c", c=C)
-                if c in y_on_vector(b):
-                    nc.vector.tensor_copy(out=dst, in_=src)
-                else:
-                    nc.scalar.copy(out=dst, in_=src)
-                if last:
-                    nc.sync.dma_start(
-                        out=out_rows[b][:, c * D : (c + 1) * D],
-                        in_=y_sb[:, c * D : (c + 1) * D],
-                    )
-            if not last:
+            st[b]["xi"] = xi
+
+        def tf(b):
+            st[b]["ti"] = [transpose_half(b, st[b]["xi"], h) for h in range(2)]
+
+        def gi(b):
+            xi_g = grp.tile([P, D * 4], BF16, name="xi_g", align_bytes=64)
+            st[b]["xi_g"] = xi_g
+            for h in range(2):
+                group_half(True, xi_g, st[b]["ti"][h], h)
+
+        def mx(b, c):
+            s = st[b]
+            if c == 0:
+                s["y"] = ysb.tile([P, C * D], F32, name="y_sb")
+                s["yp"] = {}
+            y_ps = ps_y.tile([P, D], F32, name="y_ps")
+            nc.tensor.matmul_mx(
+                out=y_ps[:],
+                lhsT=s["xi_q"][0][:, c * P : (c + 1) * P].bitcast(FP8X4),
+                lhsT_scale=s["xi_q"][1][:, c * P : (c + 1) * P],
+                rhs=s["x_q"][0][:].bitcast(FP8X4),
+                rhs_scale=s["x_q"][1][:],
+                start=True,
+                stop=True,
+            )
+            s["yp"][c] = y_ps
+
+        def y_out(b, c):
+            y_sb = st[b]["y"]
+            copy(
+                y_on_vector(b, c),
+                y_sb[:, c * D : (c + 1) * D].rearrange("p (r c) -> p r c", c=C),
+                st[b]["yp"][c][:].rearrange("p (c r) -> p r c", c=C),
+            )
+            if b == B - 1:
+                nc.sync.dma_start(out=out_rows[b][:, c * D : (c + 1) * D], in_=y_sb[:, c * D : (c + 1) * D])
+            elif c == C - 1:
                 nc.sync.dma_start(out=out_rows[b], in_=y_sb[:])
 
-        for j in range(-2, B + 1):
-            if 0 <= j + 3 < B:
-                pool_sums(j + 3)
-            if j == -2:
-                for b in range(3 - 2):
-                    pool_sums(b)
-            if j + 2 < B:
-                transposes(j + 2)
-            if 0 <= j + 1 < B:
-                spread_sums(j + 1)
-            if 0 <= j < B:
-                centre(j)
-            if j + 2 < B:
-                sums_a(j + 2)
-            if 0 <= j < B:
-                quantise(j, "x_g", "xc", "xs")
-            if j + 2 < B:
-                sums_b(j + 2)
-            if 0 <= j < B:
-                quantise(j, "xi_g", "xic", "xis")
-            if 0 <= j - 1 < B:
-                multiply(j - 1)
+        def at(b):
+            return 0 <= b < B
+
+        for j in range(-2, B):
+            a, f = j + 2, j + 1
+            if at(a):
+                ta(a)
+            if at(f):
+                centre(f)
+                tf(f)
+                quantise(f, st[f]["x_g"], "x_q")
+            if at(a):
+                bx(a)
+            if at(f):
+                gi(f)
+            if at(j):
+                mx(j, 0)
+                mx(j, 1)
+                y_out(j, 0)
+                y_out(j, 1)
+            if at(a):
+                means(a)
+                mean_copy(a)
+            if at(j):
+                mx(j, 2)
+                mx(j, 3)
+                y_out(j, 2)
+                y_out(j, 3)
+            if at(f):
+                quantise(f, st[f]["xi_g"], "xi_q")

@@ -24,8 +24,12 @@ def x_on_vector(b, h):
     return b < 2 and h == 1
 
 
+def xi_on_vector(b, h):
+    return h == 0
+
+
 def y_on_vector(b, c):
-    return c == 3 and (b % 2 == 1) or (b == B - 1 and c == 1)
+    return b == B - 1 and c % 2 == 1
 
 
 def tile_covpool_pa_kernel(tc, x, out):
@@ -39,16 +43,14 @@ def tile_covpool_pa_kernel(tc, x, out):
         grp = ctx.enter_context(tc.tile_pool(name="grp", bufs=3))
         cod = ctx.enter_context(tc.tile_pool(name="cod", bufs=3))
         small = ctx.enter_context(tc.tile_pool(name="small", bufs=4))
+        junk = ctx.enter_context(tc.tile_pool(name="junk", bufs=2))
         ysb = ctx.enter_context(tc.tile_pool(name="ysb", bufs=4))
         ps_t = ctx.enter_context(tc.psum_pool(name="ps_t", bufs=4))
-        ps_s = ctx.enter_context(tc.psum_pool(name="ps_s", bufs=1))
-        ps_y = ctx.enter_context(tc.psum_pool(name="ps_y", bufs=3))
+        ps_y = ctx.enter_context(tc.psum_pool(name="ps_y", bufs=4))
         ctx.enter_context(tc.manual_schedule())
 
         ident = const.tile([P, P], F32, name="ident")
         masks.make_identity(nc, ident[:])
-        inv_m = const.tile([P, 2], BF16, name="inv_m")
-        nc.vector.memset(inv_m[:], INV_M)
 
         x_sb = []
         for b in range(B):
@@ -67,7 +69,7 @@ def tile_covpool_pa_kernel(tc, x, out):
             else:
                 nc.scalar.copy(out=dst, in_=src)
 
-        def transpose_half(b, src, h):
+        def transpose_half(src, h):
             tp = ps_t.tile([P, 4, P], F32, name="tp")
             sw = src[:].bitcast(F32)
             for k in range(4):
@@ -85,64 +87,65 @@ def tile_covpool_pa_kernel(tc, x, out):
         def quantise(b, src, name):
             codes = cod.tile([P, D], U32, name=name + "c", align_bytes=64)
             scales = cod.tile([P, D], U8, name=name + "s", align_bytes=64)
-            nc.vector.quantize_mx(out=codes[:].bitcast(FP8X4), scales=scales[:], in_=src[:])
+            nc.vector.quantize_mx(out=codes[:].bitcast(FP8X4), scales=scales[:], in_=st[b][src][:])
             st[b][name] = (codes, scales)
 
-        def ta(b):
-            st[b]["tx"] = [transpose_half(b, x_sb[b], h) for h in range(2)]
+        def qx(b):
+            if at(b):
+                quantise(b, "x_g", "x_q")
 
-        def bx(b):
-            x_g = grp.tile([P, D * 4], BF16, name="x_g", align_bytes=64)
-            st[b]["x_g"] = x_g
-            for h in range(2):
-                group_half(x_on_vector(b, h), x_g, st[b]["tx"][h], h)
+        def qi(b):
+            if at(b):
+                quantise(b, "xi_g", "xi_q")
 
-        def means(b):
-            ms = ps_s.tile([P, C], F32, name="ms")
-            xv = st[b]["x_g"][:].rearrange("p (n t) -> p n t", t=4)
-            for c in range(C):
-                for t in range(4):
-                    nc.tensor.matmul(
-                        ms[:, c : c + 1],
-                        lhsT=xv[:, c * P : (c + 1) * P, t],
-                        rhs=inv_m[:, 0:1],
-                        start=(t == 0),
-                        stop=(t == 3),
-                    )
-            st[b]["ms"] = ms
+        def ta(b, h):
+            if at(b):
+                st[b]["tx", h] = transpose_half(x_sb[b], h)
 
-        def mean_copy(b):
-            mean = small.tile([P, C], F32, name="mean")
-            nc.scalar.copy(out=mean[:], in_=st[b]["ms"][:])
-            st[b]["mean"] = mean
+        def bx(b, h):
+            if at(b):
+                if h == 0:
+                    st[b]["x_g"] = grp.tile([P, D * 4], BF16, name="x_g", align_bytes=64)
+                group_half(x_on_vector(b, h), st[b]["x_g"], st[b]["tx", h], h)
 
-        def centre(b):
-            xi = grp.tile([P, C * M], BF16, name="xi")
-            for c in range(C):
+        def sums(b, c):
+            if at(b):
+                if "mean" not in st[b]:
+                    st[b]["mean"] = small.tile([P, C], F32, name="mean")
+                jv = junk.tile([P, M], BF16, name="jv")
                 nc.vector.tensor_scalar(
-                    out=xi[:, c * M : (c + 1) * M],
+                    out=jv[:], in0=x_sb[b][:, c * M : (c + 1) * M], scalar1=INV_M, scalar2=None,
+                    op0=ALU.mult, op1=ALU.add, accum_out=st[b]["mean"][:, c : c + 1],
+                )
+
+        def centre(b, c):
+            if at(b):
+                if "xi" not in st[b]:
+                    st[b]["xi"] = grp.tile([P, C * M], BF16, name="xi")
+                mean = st[b]["mean"]
+                nc.vector.tensor_scalar(
+                    out=st[b]["xi"][:, c * M : (c + 1) * M],
                     in0=x_sb[b][:, c * M : (c + 1) * M],
-                    scalar1=st[b]["mean"][:, c : c + 1],
+                    scalar1=mean[:, c : c + 1],
                     scalar2=INV_M,
                     op0=ALU.subtract,
                     op1=ALU.mult,
                 )
-            st[b]["xi"] = xi
 
-        def tf(b):
-            st[b]["ti"] = [transpose_half(b, st[b]["xi"], h) for h in range(2)]
+        def tf(b, h):
+            if at(b):
+                st[b]["ti", h] = transpose_half(st[b]["xi"], h)
 
-        def gi(b):
-            xi_g = grp.tile([P, D * 4], BF16, name="xi_g", align_bytes=64)
-            st[b]["xi_g"] = xi_g
-            for h in range(2):
-                group_half(True, xi_g, st[b]["ti"][h], h)
+        def gi(b, h):
+            if at(b):
+                if h == 0:
+                    st[b]["xi_g"] = grp.tile([P, D * 4], BF16, name="xi_g", align_bytes=64)
+                group_half(xi_on_vector(b, h), st[b]["xi_g"], st[b]["ti", h], h)
 
         def mx(b, c):
+            if not at(b):
+                return
             s = st[b]
-            if c == 0:
-                s["y"] = ysb.tile([P, C * D], F32, name="y_sb")
-                s["yp"] = {}
             y_ps = ps_y.tile([P, D], F32, name="y_ps")
             nc.tensor.matmul_mx(
                 out=y_ps[:],
@@ -153,18 +156,24 @@ def tile_covpool_pa_kernel(tc, x, out):
                 start=True,
                 stop=True,
             )
-            s["yp"][c] = y_ps
+            s["yp", c] = y_ps
 
         def y_out(b, c):
+            if not at(b):
+                return
+            if c == 0:
+                st[b]["y"] = ysb.tile([P, C * D], F32, name="y_sb")
             y_sb = st[b]["y"]
             copy(
                 y_on_vector(b, c),
                 y_sb[:, c * D : (c + 1) * D].rearrange("p (r c) -> p r c", c=C),
-                st[b]["yp"][c][:].rearrange("p (c r) -> p r c", c=C),
+                st[b]["yp", c][:].rearrange("p (c r) -> p r c", c=C),
             )
             if b == B - 1:
                 nc.sync.dma_start(out=out_rows[b][:, c * D : (c + 1) * D], in_=y_sb[:, c * D : (c + 1) * D])
-            elif c == C - 1:
+            elif b == B - 2 and c % 2 == 1:
+                nc.sync.dma_start(out=out_rows[b][:, (c - 1) * D : (c + 1) * D], in_=y_sb[:, (c - 1) * D : (c + 1) * D])
+            elif b < B - 2 and c == C - 1:
                 nc.sync.dma_start(out=out_rows[b], in_=y_sb[:])
 
         def at(b):
@@ -172,28 +181,21 @@ def tile_covpool_pa_kernel(tc, x, out):
 
         for j in range(-2, B):
             a, f = j + 2, j + 1
-            if at(a):
-                ta(a)
-            if at(f):
-                centre(f)
-                tf(f)
-                quantise(f, st[f]["x_g"], "x_q")
-            if at(a):
-                bx(a)
-            if at(f):
-                gi(f)
-            if at(j):
-                mx(j, 0)
-                mx(j, 1)
-                y_out(j, 0)
-                y_out(j, 1)
-            if at(a):
-                means(a)
-                mean_copy(a)
-            if at(j):
-                mx(j, 2)
-                mx(j, 3)
-                y_out(j, 2)
-                y_out(j, 3)
-            if at(f):
-                quantise(f, st[f]["xi_g"], "xi_q")
+            for h in range(2):
+                tf(f, h)
+            for h in range(2):
+                ta(a, h)
+            for c in range(C):
+                sums(a, c)
+            gi(f, 0)
+            gi(f, 1)
+            qx(f)
+            bx(a, 0)
+            bx(a, 1)
+            for c in range(C):
+                centre(a, c)
+            for c in range(C):
+                mx(j, c)
+            for c in range(C):
+                y_out(j, c)
+            qi(f)

@@ -18,18 +18,20 @@ C = D // P
 FLOPS = 2 * B * D * D * M
 
 INV_M = 1.0 / M
+YLAG = 2
+PE_CHUNKS = (0,)
 
 
 def x_on_vector(b, h):
-    return b < 2 and h == 1
+    return False
 
 
 def xi_on_vector(b, h):
-    return h == 0
+    return h == (1 if b == 0 else 0)
 
 
 def y_on_vector(b, c):
-    return b == B - 1 and c % 2 == 1
+    return c == 3 and (b % 2 == 1) or (b == B - 1 and c % 2 == 1)
 
 
 def tile_covpool_pa_kernel(tc, x, out):
@@ -46,11 +48,14 @@ def tile_covpool_pa_kernel(tc, x, out):
         junk = ctx.enter_context(tc.tile_pool(name="junk", bufs=2))
         ysb = ctx.enter_context(tc.tile_pool(name="ysb", bufs=4))
         ps_t = ctx.enter_context(tc.psum_pool(name="ps_t", bufs=4))
-        ps_y = ctx.enter_context(tc.psum_pool(name="ps_y", bufs=4))
+        ps_s = ctx.enter_context(tc.psum_pool(name="ps_s", bufs=1))
+        ps_y = ctx.enter_context(tc.psum_pool(name="ps_y", bufs=3))
         ctx.enter_context(tc.manual_schedule())
 
         ident = const.tile([P, P], F32, name="ident")
         masks.make_identity(nc, ident[:])
+        inv_m = const.tile([P, 2], BF16, name="inv_m")
+        nc.vector.memset(inv_m[:], INV_M)
 
         x_sb = []
         for b in range(B):
@@ -98,6 +103,19 @@ def tile_covpool_pa_kernel(tc, x, out):
             if at(b):
                 quantise(b, "xi_g", "xi_q")
 
+        def qi_half(b, h):
+            s = st[b]
+            if h == 0:
+                codes = cod.tile([P, D], U32, name="xi_qc", align_bytes=64)
+                scales = cod.tile([P, D], U8, name="xi_qs", align_bytes=64)
+                s["xi_q"] = (codes, scales)
+            lo, hi = h * D // 2, (h + 1) * D // 2
+            nc.vector.quantize_mx(
+                out=s["xi_q"][0][:, lo:hi].bitcast(FP8X4),
+                scales=s["xi_q"][1][:, lo:hi],
+                in_=s["xi_g"][:, 4 * lo : 4 * hi],
+            )
+
         def ta(b, h):
             if at(b):
                 st[b]["tx", h] = transpose_half(x_sb[b], h)
@@ -109,7 +127,7 @@ def tile_covpool_pa_kernel(tc, x, out):
                 group_half(x_on_vector(b, h), st[b]["x_g"], st[b]["tx", h], h)
 
         def sums(b, c):
-            if at(b):
+            if at(b) and (b < 2 or c not in PE_CHUNKS):
                 if "mean" not in st[b]:
                     st[b]["mean"] = small.tile([P, C], F32, name="mean")
                 jv = junk.tile([P, M], BF16, name="jv")
@@ -118,11 +136,27 @@ def tile_covpool_pa_kernel(tc, x, out):
                     op0=ALU.mult, op1=ALU.add, accum_out=st[b]["mean"][:, c : c + 1],
                 )
 
+        def pe_means(b):
+            if not at(b) or b < 2:
+                return
+            ms = ps_s.tile([P, C], F32, name="ms")
+            xv = st[b]["x_g"][:].rearrange("p (n t) -> p n t", t=4)
+            for c in PE_CHUNKS:
+                for t in range(4):
+                    nc.tensor.matmul(
+                        ms[:, c : c + 1],
+                        lhsT=xv[:, c * P : (c + 1) * P, t],
+                        rhs=inv_m[:, 0:1],
+                        start=(t == 0),
+                        stop=(t == 3),
+                    )
+            st[b]["ms"] = ms
+
         def centre(b, c):
             if at(b):
                 if "xi" not in st[b]:
                     st[b]["xi"] = grp.tile([P, C * M], BF16, name="xi")
-                mean = st[b]["mean"]
+                mean = st[b]["ms"] if c in PE_CHUNKS and b > 1 and b > 1 else st[b]["mean"]
                 nc.vector.tensor_scalar(
                     out=st[b]["xi"][:, c * M : (c + 1) * M],
                     in0=x_sb[b][:, c * M : (c + 1) * M],
@@ -176,26 +210,58 @@ def tile_covpool_pa_kernel(tc, x, out):
             elif b < B - 2 and c == C - 1:
                 nc.sync.dma_start(out=out_rows[b], in_=y_sb[:])
 
+        def multiply(b):
+            for c in range(C):
+                mx(b, c)
+                if c >= YLAG:
+                    y_out(b, c - YLAG)
+            for c in range(C - YLAG, C):
+                y_out(b, c)
+
         def at(b):
             return 0 <= b < B
 
-        for j in range(-2, B):
+        for h in range(2):
+            ta(0, h)
+            bx(0, h)
+        for h in range(2):
+            for c in (2 * h, 2 * h + 1):
+                sums(0, c)
+            for c in (2 * h, 2 * h + 1):
+                centre(0, c)
+            tf(0, h)
+        gi(0, 0)
+        qx(0)
+        gi(0, 1)
+        for h in range(2):
+            ta(1, h)
+            bx(1, h)
+        sums(1, 0)
+        qi(0)
+        for c in range(1, C):
+            sums(1, c)
+        for j in range(0, B):
             a, f = j + 2, j + 1
-            for h in range(2):
-                tf(f, h)
+            if j == 0:
+                multiply(j)
             for h in range(2):
                 ta(a, h)
             for c in range(C):
+                centre(f, c)
+            tf(f, 0)
+            tf(f, 1)
+            for c in range(C):
                 sums(a, c)
             gi(f, 0)
-            gi(f, 1)
             qx(f)
             bx(a, 0)
             bx(a, 1)
-            for c in range(C):
-                centre(a, c)
-            for c in range(C):
-                mx(j, c)
-            for c in range(C):
-                y_out(j, c)
-            qi(f)
+            pe_means(a)
+            gi(f, 1)
+            if j == B - 2:
+                qi_half(f, 0)
+                qi_half(f, 1)
+            else:
+                qi(f)
+            if j > 0:
+                multiply(j)

@@ -18,8 +18,7 @@ C = D // P
 FLOPS = 2 * B * D * D * M
 
 INV_M = 1.0 / M
-YLAG = 2
-PE_CHUNKS = (0,)
+PE_CHUNKS = (0, 1,)
 
 
 def x_on_vector(b, h):
@@ -27,11 +26,11 @@ def x_on_vector(b, h):
 
 
 def xi_on_vector(b, h):
-    return h == (1 if b == 0 else 0)
+    return h == 1 if b == 0 else h == 0 or b % 3 != 2
 
 
 def y_on_vector(b, c):
-    return c == 3 and (b % 2 == 1) or (b == B - 1 and c % 2 == 1)
+    return b == B - 1 and c % 2 == 1
 
 
 def tile_covpool_pa_kernel(tc, x, out):
@@ -42,7 +41,7 @@ def tile_covpool_pa_kernel(tc, x, out):
     with ExitStack() as ctx:
         const = ctx.enter_context(tc.tile_pool(name="const", bufs=1))
         xin = ctx.enter_context(tc.tile_pool(name="xin", bufs=1))
-        grp = ctx.enter_context(tc.tile_pool(name="grp", bufs=3))
+        grp = ctx.enter_context(tc.tile_pool(name="grp", bufs=4))
         cod = ctx.enter_context(tc.tile_pool(name="cod", bufs=3))
         small = ctx.enter_context(tc.tile_pool(name="small", bufs=4))
         junk = ctx.enter_context(tc.tile_pool(name="junk", bufs=2))
@@ -156,7 +155,7 @@ def tile_covpool_pa_kernel(tc, x, out):
             if at(b):
                 if "xi" not in st[b]:
                     st[b]["xi"] = grp.tile([P, C * M], BF16, name="xi")
-                mean = st[b]["ms"] if c in PE_CHUNKS and b > 1 and b > 1 else st[b]["mean"]
+                mean = st[b]["ms"] if c in PE_CHUNKS and b >= 2 else st[b]["mean"]
                 nc.vector.tensor_scalar(
                     out=st[b]["xi"][:, c * M : (c + 1) * M],
                     in0=x_sb[b][:, c * M : (c + 1) * M],
@@ -170,9 +169,9 @@ def tile_covpool_pa_kernel(tc, x, out):
             if at(b):
                 st[b]["ti", h] = transpose_half(st[b]["xi"], h)
 
-        def gi(b, h):
+        def gi(b, h, first=False):
             if at(b):
-                if h == 0:
+                if h == 0 and "xi_g" not in st[b] or first:
                     st[b]["xi_g"] = grp.tile([P, D * 4], BF16, name="xi_g", align_bytes=64)
                 group_half(xi_on_vector(b, h), st[b]["xi_g"], st[b]["ti", h], h)
 
@@ -210,14 +209,6 @@ def tile_covpool_pa_kernel(tc, x, out):
             elif b < B - 2 and c == C - 1:
                 nc.sync.dma_start(out=out_rows[b], in_=y_sb[:])
 
-        def multiply(b):
-            for c in range(C):
-                mx(b, c)
-                if c >= YLAG:
-                    y_out(b, c - YLAG)
-            for c in range(C - YLAG, C):
-                y_out(b, c)
-
         def at(b):
             return 0 <= b < B
 
@@ -233,35 +224,44 @@ def tile_covpool_pa_kernel(tc, x, out):
         gi(0, 0)
         qx(0)
         gi(0, 1)
-        for h in range(2):
-            ta(1, h)
-            bx(1, h)
+        for b in (1, 2):
+            for h in range(2):
+                ta(b, h)
+                bx(b, h)
         sums(1, 0)
         qi(0)
         for c in range(1, C):
             sums(1, c)
+        for c in range(C):
+            centre(1, c)
         for j in range(0, B):
-            a, f = j + 2, j + 1
-            if j == 0:
-                multiply(j)
-            for h in range(2):
-                ta(a, h)
-            for c in range(C):
-                centre(f, c)
-            tf(f, 0)
-            tf(f, 1)
-            for c in range(C):
-                sums(a, c)
-            gi(f, 0)
-            qx(f)
-            bx(a, 0)
-            bx(a, 1)
-            pe_means(a)
-            gi(f, 1)
-            if j == B - 2:
-                qi_half(f, 0)
-                qi_half(f, 1)
-            else:
-                qi(f)
             if j > 0:
-                multiply(j)
+                qi(j)
+                for h in range(2):
+                    tf(j + 1, h)
+            mx(j, 0)
+            mx(j, 1)
+            mx(j, 2)
+            if j > 0 and not xi_on_vector(j + 1, 1):
+                gi(j + 1, 1, True)
+            y_out(j, 0)
+            pe_means(j + 2)
+            mx(j, 3)
+            if j == 0:
+                for h in range(2):
+                    tf(j + 1, h)
+            for h in range(2):
+                ta(j + 3, h)
+            for c in range(C):
+                sums(j + 2, c)
+            qx(j + 1)
+            gi(j + 1, 0)
+            if j == 0 or xi_on_vector(j + 1, 1):
+                gi(j + 1, 1)
+            y_out(j, 1)
+            y_out(j, 2)
+            y_out(j, 3)
+            for h in range(2):
+                bx(j + 3, h)
+            for c in range(C):
+                centre(j + 2, c)

@@ -18,7 +18,7 @@ C = D // P
 FLOPS = 2 * B * D * D * M
 
 INV_M = 1.0 / M
-PE_CHUNKS = (0, 1,)
+PE_CHUNKS = (0, 1, 2,)
 
 
 def x_on_vector(b, h):
@@ -26,7 +26,7 @@ def x_on_vector(b, h):
 
 
 def xi_on_vector(b, h):
-    return h == 1 if b == 0 else h == 0 or b % 3 != 2
+    return h == 1 if b == 0 else True
 
 
 def y_on_vector(b, c):
@@ -202,11 +202,11 @@ def tile_covpool_pa_kernel(tc, x, out):
                 y_sb[:, c * D : (c + 1) * D].rearrange("p (r c) -> p r c", c=C),
                 st[b]["yp", c][:].rearrange("p (c r) -> p r c", c=C),
             )
-            if b == B - 1:
+            if b >= B - 1:
                 nc.sync.dma_start(out=out_rows[b][:, c * D : (c + 1) * D], in_=y_sb[:, c * D : (c + 1) * D])
-            elif b == B - 2 and c % 2 == 1:
+            elif b >= B - 4 and c % 2 == 1:
                 nc.sync.dma_start(out=out_rows[b][:, (c - 1) * D : (c + 1) * D], in_=y_sb[:, (c - 1) * D : (c + 1) * D])
-            elif b < B - 2 and c == C - 1:
+            elif b < B - 4 and c == C - 1:
                 nc.sync.dma_start(out=out_rows[b], in_=y_sb[:])
 
         def at(b):

@@ -26,7 +26,7 @@ def x_on_vector(b, h):
 
 
 def xi_on_vector(b, h):
-    return h == 1 if b == 0 else True
+    return h == (1 if b == 0 else 0) or b > 1
 
 
 def y_on_vector(b, c):
@@ -126,7 +126,7 @@ def tile_covpool_pa_kernel(tc, x, out):
                 group_half(x_on_vector(b, h), st[b]["x_g"], st[b]["tx", h], h)
 
         def sums(b, c):
-            if at(b) and (b < 2 or c not in PE_CHUNKS):
+            if at(b) and (b < 1 or c not in PE_CHUNKS):
                 if "mean" not in st[b]:
                     st[b]["mean"] = small.tile([P, C], F32, name="mean")
                 jv = junk.tile([P, M], BF16, name="jv")
@@ -136,7 +136,7 @@ def tile_covpool_pa_kernel(tc, x, out):
                 )
 
         def pe_means(b):
-            if not at(b) or b < 2:
+            if not at(b) or b < 1:
                 return
             ms = ps_s.tile([P, C], F32, name="ms")
             xv = st[b]["x_g"][:].rearrange("p (n t) -> p n t", t=4)
@@ -155,7 +155,7 @@ def tile_covpool_pa_kernel(tc, x, out):
             if at(b):
                 if "xi" not in st[b]:
                     st[b]["xi"] = grp.tile([P, C * M], BF16, name="xi")
-                mean = st[b]["ms"] if c in PE_CHUNKS and b >= 2 else st[b]["mean"]
+                mean = st[b]["ms"] if c in PE_CHUNKS and b >= 1 else st[b]["mean"]
                 nc.vector.tensor_scalar(
                     out=st[b]["xi"][:, c * M : (c + 1) * M],
                     in0=x_sb[b][:, c * M : (c + 1) * M],
@@ -202,9 +202,7 @@ def tile_covpool_pa_kernel(tc, x, out):
                 y_sb[:, c * D : (c + 1) * D].rearrange("p (r c) -> p r c", c=C),
                 st[b]["yp", c][:].rearrange("p (c r) -> p r c", c=C),
             )
-            if b >= B - 1:
-                nc.sync.dma_start(out=out_rows[b][:, c * D : (c + 1) * D], in_=y_sb[:, c * D : (c + 1) * D])
-            elif b >= B - 4 and c % 2 == 1:
+            if b >= B - 4 and c % 2 == 1:
                 nc.sync.dma_start(out=out_rows[b][:, (c - 1) * D : (c + 1) * D], in_=y_sb[:, (c - 1) * D : (c + 1) * D])
             elif b < B - 4 and c == C - 1:
                 nc.sync.dma_start(out=out_rows[b], in_=y_sb[:])
@@ -223,45 +221,61 @@ def tile_covpool_pa_kernel(tc, x, out):
             tf(0, h)
         gi(0, 0)
         qx(0)
+        qi_half(0, 0)
         gi(0, 1)
-        for b in (1, 2):
-            for h in range(2):
-                ta(b, h)
-                bx(b, h)
-        sums(1, 0)
-        qi(0)
-        for c in range(1, C):
+        for h in range(2):
+            ta(1, h)
+            bx(1, h)
+        for c in range(C):
             sums(1, c)
+        qi_half(0, 1)
+        mx(0, 0)
+        mx(0, 1)
+        y_out(0, 0)
+        y_out(0, 1)
+        ta(2, 0)
+        ta(2, 1)
+        pe_means(1)
+        bx(2, 0)
+        bx(2, 1)
+        qx(1)
+        for c in range(C):
+            sums(2, c)
         for c in range(C):
             centre(1, c)
+        mx(0, 2)
+        mx(0, 3)
+        y_out(0, 2)
+        y_out(0, 3)
         for j in range(0, B):
-            if j > 0:
+            if j == B - 1:
+                qi_half(j, 0)
+                qi_half(j, 1)
+            elif j > 0:
                 qi(j)
-                for h in range(2):
-                    tf(j + 1, h)
-            mx(j, 0)
-            mx(j, 1)
-            mx(j, 2)
-            if j > 0 and not xi_on_vector(j + 1, 1):
-                gi(j + 1, 1, True)
-            y_out(j, 0)
+            tf(j + 1, 0)
+            tf(j + 1, 1)
+            if j > 0:
+                mx(j, 0)
+                mx(j, 1)
+                mx(j, 2)
+                y_out(j, 0)
             pe_means(j + 2)
-            mx(j, 3)
-            if j == 0:
-                for h in range(2):
-                    tf(j + 1, h)
-            for h in range(2):
-                ta(j + 3, h)
-            for c in range(C):
-                sums(j + 2, c)
-            qx(j + 1)
+            if j > 0:
+                mx(j, 3)
+            ta(j + 3, 0)
+            ta(j + 3, 1)
+            if j > 0:
+                for c in range(C):
+                    sums(j + 2, c)
+                qx(j + 1)
             gi(j + 1, 0)
-            if j == 0 or xi_on_vector(j + 1, 1):
-                gi(j + 1, 1)
-            y_out(j, 1)
-            y_out(j, 2)
-            y_out(j, 3)
-            for h in range(2):
-                bx(j + 3, h)
+            if j > 0:
+                y_out(j, 1)
+                y_out(j, 2)
+                y_out(j, 3)
+            gi(j + 1, 1)
+            bx(j + 3, 0)
+            bx(j + 3, 1)
             for c in range(C):
                 centre(j + 2, c)

@@ -18,6 +18,7 @@ C = D // P
 FLOPS = 2 * B * D * D * M
 
 INV_M = 1.0 / M
+MEAN_N = 8
 PE_CHUNKS = (0, 1, 2,)
 
 
@@ -53,7 +54,7 @@ def tile_covpool_pa_kernel(tc, x, out):
 
         ident = const.tile([P, P], F32, name="ident")
         masks.make_identity(nc, ident[:])
-        inv_m = const.tile([P, 2], BF16, name="inv_m")
+        inv_m = const.tile([P, MEAN_N], BF16, name="inv_m")
         nc.vector.memset(inv_m[:], INV_M)
 
         x_sb = []
@@ -138,14 +139,14 @@ def tile_covpool_pa_kernel(tc, x, out):
         def pe_means(b):
             if not at(b) or b < 1:
                 return
-            ms = ps_s.tile([P, C], F32, name="ms")
+            ms = ps_s.tile([P, C, MEAN_N], F32, name="ms")
             xv = st[b]["x_g"][:].rearrange("p (n t) -> p n t", t=4)
             for c in PE_CHUNKS:
                 for t in range(4):
                     nc.tensor.matmul(
-                        ms[:, c : c + 1],
+                        ms[:, c, :],
                         lhsT=xv[:, c * P : (c + 1) * P, t],
-                        rhs=inv_m[:, 0:1],
+                        rhs=inv_m[:],
                         start=(t == 0),
                         stop=(t == 3),
                     )
@@ -155,11 +156,14 @@ def tile_covpool_pa_kernel(tc, x, out):
             if at(b):
                 if "xi" not in st[b]:
                     st[b]["xi"] = grp.tile([P, C * M], BF16, name="xi")
-                mean = st[b]["ms"] if c in PE_CHUNKS and b >= 1 else st[b]["mean"]
+                if c in PE_CHUNKS and b >= 1:
+                    mean = st[b]["ms"][:, c, 0:1]
+                else:
+                    mean = st[b]["mean"][:, c : c + 1]
                 nc.vector.tensor_scalar(
                     out=st[b]["xi"][:, c * M : (c + 1) * M],
                     in0=x_sb[b][:, c * M : (c + 1) * M],
-                    scalar1=mean[:, c : c + 1],
+                    scalar1=mean,
                     scalar2=INV_M,
                     op0=ALU.subtract,
                     op1=ALU.mult,

@@ -27,7 +27,7 @@ def x_on_vector(b, h):
 
 
 def xi_on_vector(b, h):
-    return h == (1 if b == 0 else 0) or b > 1
+    return h == 0 or b < B - 2
 
 
 def y_on_vector(b, c):
@@ -42,14 +42,12 @@ def tile_covpool_pa_kernel(tc, x, out):
     with ExitStack() as ctx:
         const = ctx.enter_context(tc.tile_pool(name="const", bufs=1))
         xin = ctx.enter_context(tc.tile_pool(name="xin", bufs=1))
-        grp = ctx.enter_context(tc.tile_pool(name="grp", bufs=4))
+        grp = ctx.enter_context(tc.tile_pool(name="grp", bufs=7))
         cod = ctx.enter_context(tc.tile_pool(name="cod", bufs=3))
         small = ctx.enter_context(tc.tile_pool(name="small", bufs=4))
         junk = ctx.enter_context(tc.tile_pool(name="junk", bufs=2))
         ysb = ctx.enter_context(tc.tile_pool(name="ysb", bufs=4))
-        ps_t = ctx.enter_context(tc.psum_pool(name="ps_t", bufs=4))
-        ps_s = ctx.enter_context(tc.psum_pool(name="ps_s", bufs=1))
-        ps_y = ctx.enter_context(tc.psum_pool(name="ps_y", bufs=3))
+        psum = ctx.enter_context(tc.psum_pool(name="psum", bufs=8))
         ctx.enter_context(tc.manual_schedule())
 
         ident = const.tile([P, P], F32, name="ident")
@@ -75,7 +73,7 @@ def tile_covpool_pa_kernel(tc, x, out):
                 nc.scalar.copy(out=dst, in_=src)
 
         def transpose_half(src, h):
-            tp = ps_t.tile([P, 4, P], F32, name="tp")
+            tp = psum.tile([P, 4, P], F32, name="tp", tag="bank")
             sw = src[:].bitcast(F32)
             for k in range(4):
                 col = (4 * h + k) * P
@@ -103,19 +101,6 @@ def tile_covpool_pa_kernel(tc, x, out):
             if at(b):
                 quantise(b, "xi_g", "xi_q")
 
-        def qi_half(b, h):
-            s = st[b]
-            if h == 0:
-                codes = cod.tile([P, D], U32, name="xi_qc", align_bytes=64)
-                scales = cod.tile([P, D], U8, name="xi_qs", align_bytes=64)
-                s["xi_q"] = (codes, scales)
-            lo, hi = h * D // 2, (h + 1) * D // 2
-            nc.vector.quantize_mx(
-                out=s["xi_q"][0][:, lo:hi].bitcast(FP8X4),
-                scales=s["xi_q"][1][:, lo:hi],
-                in_=s["xi_g"][:, 4 * lo : 4 * hi],
-            )
-
         def ta(b, h):
             if at(b):
                 st[b]["tx", h] = transpose_half(x_sb[b], h)
@@ -139,7 +124,8 @@ def tile_covpool_pa_kernel(tc, x, out):
         def pe_means(b):
             if not at(b) or b < 1:
                 return
-            ms = ps_s.tile([P, C, MEAN_N], F32, name="ms")
+            ms_bank = psum.tile([P, D], F32, name="ms", tag="bank")
+            ms = ms_bank[:, : C * MEAN_N].rearrange("p (c n) -> p c n", c=C)
             xv = st[b]["x_g"][:].rearrange("p (n t) -> p n t", t=4)
             for c in PE_CHUNKS:
                 for t in range(4):
@@ -183,7 +169,7 @@ def tile_covpool_pa_kernel(tc, x, out):
             if not at(b):
                 return
             s = st[b]
-            y_ps = ps_y.tile([P, D], F32, name="y_ps")
+            y_ps = psum.tile([P, D], F32, name="y_ps", tag="bank")
             nc.tensor.matmul_mx(
                 out=y_ps[:],
                 lhsT=s["xi_q"][0][:, c * P : (c + 1) * P].bitcast(FP8X4),
@@ -206,7 +192,9 @@ def tile_covpool_pa_kernel(tc, x, out):
                 y_sb[:, c * D : (c + 1) * D].rearrange("p (r c) -> p r c", c=C),
                 st[b]["yp", c][:].rearrange("p (c r) -> p r c", c=C),
             )
-            if b >= B - 4 and c % 2 == 1:
+            if b == B - 1:
+                nc.sync.dma_start(out=out_rows[b][:, c * D : (c + 1) * D], in_=y_sb[:, c * D : (c + 1) * D])
+            elif b >= B - 4 and c % 2 == 1:
                 nc.sync.dma_start(out=out_rows[b][:, (c - 1) * D : (c + 1) * D], in_=y_sb[:, (c - 1) * D : (c + 1) * D])
             elif b < B - 4 and c == C - 1:
                 nc.sync.dma_start(out=out_rows[b], in_=y_sb[:])
@@ -222,64 +210,48 @@ def tile_covpool_pa_kernel(tc, x, out):
                 sums(0, c)
             for c in (2 * h, 2 * h + 1):
                 centre(0, c)
-            tf(0, h)
-        gi(0, 0)
-        qx(0)
-        qi_half(0, 0)
-        gi(0, 1)
         for h in range(2):
             ta(1, h)
             bx(1, h)
-        for c in range(C):
-            sums(1, c)
-        qi_half(0, 1)
-        mx(0, 0)
-        mx(0, 1)
-        y_out(0, 0)
-        y_out(0, 1)
+        tf(0, 0)
+        tf(0, 1)
+        sums(1, 3)
+        qx(0)
         ta(2, 0)
         ta(2, 1)
         pe_means(1)
         bx(2, 0)
         bx(2, 1)
-        qx(1)
-        for c in range(C):
-            sums(2, c)
+        sums(2, 3)
+        gi(0, 0)
+        gi(0, 1)
+        ta(3, 0)
+        ta(3, 1)
         for c in range(C):
             centre(1, c)
-        mx(0, 2)
-        mx(0, 3)
-        y_out(0, 2)
-        y_out(0, 3)
-        for j in range(0, B):
-            if j == B - 1:
-                qi_half(j, 0)
-                qi_half(j, 1)
-            elif j > 0:
-                qi(j)
+        pe_means(2)
+        bx(3, 0)
+        bx(3, 1)
+        ta(4, 0)
+        ta(4, 1)
+        bx(4, 0)
+        bx(4, 1)
+        for j in range(B):
+            qi(j)
             tf(j + 1, 0)
             tf(j + 1, 1)
-            if j > 0:
-                mx(j, 0)
-                mx(j, 1)
-                mx(j, 2)
-                y_out(j, 0)
-            pe_means(j + 2)
-            if j > 0:
-                mx(j, 3)
-            ta(j + 3, 0)
-            ta(j + 3, 1)
-            if j > 0:
-                for c in range(C):
-                    sums(j + 2, c)
-                qx(j + 1)
-            gi(j + 1, 0)
-            if j > 0:
-                y_out(j, 1)
-                y_out(j, 2)
-                y_out(j, 3)
-            gi(j + 1, 1)
-            bx(j + 3, 0)
-            bx(j + 3, 1)
             for c in range(C):
                 centre(j + 2, c)
+            for c in range(C):
+                mx(j, c)
+            pe_means(j + 3)
+            qx(j + 1)
+            gi(j + 1, 0)
+            gi(j + 1, 1)
+            for c in range(C):
+                y_out(j, c)
+            ta(j + 5, 0)
+            ta(j + 5, 1)
+            bx(j + 5, 0)
+            bx(j + 5, 1)
+            sums(j + 3, 3)

@@ -18,7 +18,7 @@ C = D // P
 FLOPS = 2 * B * D * D * M
 
 INV_M = 1.0 / M
-MEAN_N = 8
+MEAN_N = 64
 PE_CHUNKS = (0, 1, 2,)
 
 

@@ -52,6 +52,8 @@ def tile_covpool_pa_kernel(tc, x, out):
 
         ident = const.tile([P, P], F32, name="ident")
         masks.make_identity(nc, ident[:])
+        warm_t = const.tile([P, P], F32, name="warm_t")
+        nc.vector.memset(warm_t[:], 1.0)
         inv_m = const.tile([P, MEAN_N], BF16, name="inv_m")
         nc.vector.memset(inv_m[:], INV_M)
 
@@ -72,8 +74,12 @@ def tile_covpool_pa_kernel(tc, x, out):
             else:
                 nc.scalar.copy(out=dst, in_=src)
 
-        def transpose_half(src, h):
+        def transpose_half(src, h, warm=0):
             tp = psum.tile([P, 4, P], F32, name="tp", tag="bank")
+            for k in range(warm):
+                nc.tensor.matmul(
+                    tp[:, 0, :], lhsT=warm_t[:], rhs=warm_t[:], start=True, stop=True
+                )
             sw = src[:].bitcast(F32)
             for k in range(4):
                 col = (4 * h + k) * P
@@ -101,9 +107,9 @@ def tile_covpool_pa_kernel(tc, x, out):
             if at(b):
                 quantise(b, "xi_g", "xi_q")
 
-        def ta(b, h):
+        def ta(b, h, warm=0):
             if at(b):
-                st[b]["tx", h] = transpose_half(x_sb[b], h)
+                st[b]["tx", h] = transpose_half(x_sb[b], h, warm)
 
         def bx(b, h):
             if at(b):
@@ -155,9 +161,9 @@ def tile_covpool_pa_kernel(tc, x, out):
                     op1=ALU.mult,
                 )
 
-        def tf(b, h):
+        def tf(b, h, warm=0):
             if at(b):
-                st[b]["ti", h] = transpose_half(st[b]["xi"], h)
+                st[b]["ti", h] = transpose_half(st[b]["xi"], h, warm)
 
         def gi(b, h, first=False):
             if at(b):
@@ -192,48 +198,50 @@ def tile_covpool_pa_kernel(tc, x, out):
                 y_sb[:, c * D : (c + 1) * D].rearrange("p (r c) -> p r c", c=C),
                 st[b]["yp", c][:].rearrange("p (c r) -> p r c", c=C),
             )
-            if b == B - 1:
+            if b >= B - 2:
                 nc.sync.dma_start(out=out_rows[b][:, c * D : (c + 1) * D], in_=y_sb[:, c * D : (c + 1) * D])
-            elif b >= B - 4 and c % 2 == 1:
+            elif b >= B - 8 and c % 2 == 1:
                 nc.sync.dma_start(out=out_rows[b][:, (c - 1) * D : (c + 1) * D], in_=y_sb[:, (c - 1) * D : (c + 1) * D])
-            elif b < B - 4 and c == C - 1:
+            elif b < B - 8 and c == C - 1:
                 nc.sync.dma_start(out=out_rows[b], in_=y_sb[:])
 
         def at(b):
             return 0 <= b < B
 
-        for h in range(2):
-            ta(0, h)
-            bx(0, h)
+        ta(0, 0, 7)
+        bx(0, 0)
+        ta(0, 1, 0)
+        bx(0, 1)
         for h in range(2):
             for c in (2 * h, 2 * h + 1):
                 sums(0, c)
             for c in (2 * h, 2 * h + 1):
                 centre(0, c)
-        for h in range(2):
-            ta(1, h)
-            bx(1, h)
-        tf(0, 0)
-        tf(0, 1)
+        ta(1, 0, 2)
+        bx(1, 0)
+        ta(1, 1, 0)
+        bx(1, 1)
+        tf(0, 0, 0)
+        tf(0, 1, 0)
         sums(1, 3)
         qx(0)
-        ta(2, 0)
-        ta(2, 1)
+        ta(2, 0, 0)
+        ta(2, 1, 0)
         pe_means(1)
         bx(2, 0)
         bx(2, 1)
         sums(2, 3)
         gi(0, 0)
         gi(0, 1)
-        ta(3, 0)
-        ta(3, 1)
+        ta(3, 0, 0)
+        ta(3, 1, 0)
         for c in range(C):
             centre(1, c)
         pe_means(2)
         bx(3, 0)
         bx(3, 1)
-        ta(4, 0)
-        ta(4, 1)
+        ta(4, 0, 0)
+        ta(4, 1, 0)
         bx(4, 0)
         bx(4, 1)
         for j in range(B):
@@ -242,14 +250,18 @@ def tile_covpool_pa_kernel(tc, x, out):
             tf(j + 1, 1)
             for c in range(C):
                 centre(j + 2, c)
-            for c in range(C):
-                mx(j, c)
+            mx(j, 0)
+            mx(j, 1)
+            mx(j, 2)
+            mx(j, 3)
             pe_means(j + 3)
             qx(j + 1)
             gi(j + 1, 0)
             gi(j + 1, 1)
-            for c in range(C):
-                y_out(j, c)
+            y_out(j, 0)
+            y_out(j, 1)
+            y_out(j, 2)
+            y_out(j, 3)
             ta(j + 5, 0)
             ta(j + 5, 1)
             bx(j + 5, 0)

@@ -18,7 +18,7 @@ C = D // P
 FLOPS = 2 * B * D * D * M
 
 INV_M = 1.0 / M
-MEAN_N = 64
+MEAN_N = 32
 PE_CHUNKS = (0, 1, 2,)
 
 

@@ -19,7 +19,7 @@ FLOPS = 2 * B * D * D * M
 
 INV_M = 1.0 / M
 MEAN_N = 32
-PE_CHUNKS = (0, 1, 2,)
+PE_CHUNKS = (0, 1, 2)
 
 
 def x_on_vector(b, h):
@@ -28,6 +28,10 @@ def x_on_vector(b, h):
 
 def xi_on_vector(b, h):
     return h == 0 or b < B - 2
+
+
+def on_gpsimd(b, c):
+    return c == 3 and b >= 2
 
 
 def y_on_vector(b, c):
@@ -107,6 +111,19 @@ def tile_covpool_pa_kernel(tc, x, out):
             if at(b):
                 quantise(b, "xi_g", "xi_q")
 
+        def qi_half(b, h):
+            s = st[b]
+            if h == 0:
+                codes = cod.tile([P, D], U32, name="xi_qc", align_bytes=64)
+                scales = cod.tile([P, D], U8, name="xi_qs", align_bytes=64)
+                s["xi_q"] = (codes, scales)
+            lo, hi = h * D // 2, (h + 1) * D // 2
+            nc.vector.quantize_mx(
+                out=s["xi_q"][0][:, lo:hi].bitcast(FP8X4),
+                scales=s["xi_q"][1][:, lo:hi],
+                in_=s["xi_g"][:, 4 * lo : 4 * hi],
+            )
+
         def ta(b, h, warm=0):
             if at(b):
                 st[b]["tx", h] = transpose_half(x_sb[b], h, warm)
@@ -121,9 +138,10 @@ def tile_covpool_pa_kernel(tc, x, out):
             if at(b) and (b < 1 or c not in PE_CHUNKS):
                 if "mean" not in st[b]:
                     st[b]["mean"] = small.tile([P, C], F32, name="mean")
+                factor = -INV_M * INV_M if on_gpsimd(b, c) else INV_M
                 jv = junk.tile([P, M], BF16, name="jv")
                 nc.vector.tensor_scalar(
-                    out=jv[:], in0=x_sb[b][:, c * M : (c + 1) * M], scalar1=INV_M, scalar2=None,
+                    out=jv[:], in0=x_sb[b][:, c * M : (c + 1) * M], scalar1=factor, scalar2=None,
                     op0=ALU.mult, op1=ALU.add, accum_out=st[b]["mean"][:, c : c + 1],
                 )
 
@@ -148,6 +166,16 @@ def tile_covpool_pa_kernel(tc, x, out):
             if at(b):
                 if "xi" not in st[b]:
                     st[b]["xi"] = grp.tile([P, C * M], BF16, name="xi")
+                if on_gpsimd(b, c):
+                    nc.gpsimd.tensor_scalar(
+                        out=st[b]["xi"][:, c * M : (c + 1) * M],
+                        in0=x_sb[b][:, c * M : (c + 1) * M],
+                        scalar1=INV_M,
+                        scalar2=st[b]["mean"][:, c : c + 1],
+                        op0=ALU.mult,
+                        op1=ALU.add,
+                    )
+                    return
                 if c in PE_CHUNKS and b >= 1:
                     mean = st[b]["ms"][:, c, 0:1]
                 else:
@@ -210,54 +238,63 @@ def tile_covpool_pa_kernel(tc, x, out):
 
         ta(0, 0, 7)
         bx(0, 0)
-        ta(0, 1, 0)
+        ta(0, 1)
         bx(0, 1)
-        for h in range(2):
-            for c in (2 * h, 2 * h + 1):
-                sums(0, c)
-            for c in (2 * h, 2 * h + 1):
-                centre(0, c)
+        sums(0, 0)
+        sums(0, 1)
+        centre(0, 0)
+        centre(0, 1)
+        sums(0, 2)
+        sums(0, 3)
+        centre(0, 2)
+        centre(0, 3)
         ta(1, 0, 2)
         bx(1, 0)
-        ta(1, 1, 0)
+        ta(1, 1)
         bx(1, 1)
-        tf(0, 0, 0)
-        tf(0, 1, 0)
+        tf(0, 0)
+        tf(0, 1)
         sums(1, 3)
         qx(0)
-        ta(2, 0, 0)
-        ta(2, 1, 0)
+        gi(0, 0)
+        gi(0, 1)
+        ta(2, 0)
+        ta(2, 1)
         pe_means(1)
         bx(2, 0)
         bx(2, 1)
         sums(2, 3)
-        gi(0, 0)
-        gi(0, 1)
-        ta(3, 0, 0)
-        ta(3, 1, 0)
-        for c in range(C):
-            centre(1, c)
+        centre(2, 3)
+        ta(3, 0)
+        ta(3, 1)
+        centre(1, 0)
+        centre(1, 1)
+        centre(1, 2)
+        centre(1, 3)
         pe_means(2)
         bx(3, 0)
         bx(3, 1)
-        ta(4, 0, 0)
-        ta(4, 1, 0)
+        ta(4, 0)
+        ta(4, 1)
         bx(4, 0)
         bx(4, 1)
         for j in range(B):
             qi(j)
             tf(j + 1, 0)
             tf(j + 1, 1)
-            for c in range(C):
-                centre(j + 2, c)
+            centre(j + 2, 0)
+            centre(j + 2, 1)
+            centre(j + 2, 2)
             mx(j, 0)
             mx(j, 1)
             mx(j, 2)
             mx(j, 3)
             pe_means(j + 3)
-            qx(j + 1)
+            sums(j + 3, 3)
+            centre(j + 3, 3)
             gi(j + 1, 0)
             gi(j + 1, 1)
+            qx(j + 1)
             y_out(j, 0)
             y_out(j, 1)
             y_out(j, 2)
@@ -266,4 +303,3 @@ def tile_covpool_pa_kernel(tc, x, out):
             ta(j + 5, 1)
             bx(j + 5, 0)
             bx(j + 5, 1)
-            sums(j + 3, 3)

@@ -23,7 +23,7 @@ PE_CHUNKS = (0, 1, 2)
 
 
 def x_on_vector(b, h):
-    return False
+    return h == 0 and b > 4 and b % 5 == 1
 
 
 def xi_on_vector(b, h):
@@ -31,7 +31,7 @@ def xi_on_vector(b, h):
 
 
 def on_gpsimd(b, c):
-    return c == 3 and b >= 2
+    return c == 3 and b >= 3
 
 
 def y_on_vector(b, c):
@@ -130,7 +130,7 @@ def tile_covpool_pa_kernel(tc, x, out):
 
         def bx(b, h):
             if at(b):
-                if h == 0:
+                if "x_g" not in st[b]:
                     st[b]["x_g"] = grp.tile([P, D * 4], BF16, name="x_g", align_bytes=64)
                 group_half(x_on_vector(b, h), st[b]["x_g"], st[b]["tx", h], h)
 
@@ -264,7 +264,6 @@ def tile_covpool_pa_kernel(tc, x, out):
         bx(2, 0)
         bx(2, 1)
         sums(2, 3)
-        centre(2, 3)
         ta(3, 0)
         ta(3, 1)
         centre(1, 0)
@@ -285,13 +284,18 @@ def tile_covpool_pa_kernel(tc, x, out):
             centre(j + 2, 0)
             centre(j + 2, 1)
             centre(j + 2, 2)
+            if not on_gpsimd(j + 2, 3):
+                centre(j + 2, 3)
+            if x_on_vector(j + 4, 0):
+                bx(j + 4, 0)
             mx(j, 0)
             mx(j, 1)
             mx(j, 2)
             mx(j, 3)
             pe_means(j + 3)
             sums(j + 3, 3)
-            centre(j + 3, 3)
+            if on_gpsimd(j + 3, 3):
+                centre(j + 3, 3)
             gi(j + 1, 0)
             gi(j + 1, 1)
             qx(j + 1)
@@ -301,5 +305,6 @@ def tile_covpool_pa_kernel(tc, x, out):
             y_out(j, 3)
             ta(j + 5, 0)
             ta(j + 5, 1)
-            bx(j + 5, 0)
+            if not x_on_vector(j + 5, 0):
+                bx(j + 5, 0)
             bx(j + 5, 1)

from contextlib import ExitStack

import concourse.masks as masks
import concourse.mybir as mybir

BF16 = mybir.dt.bfloat16
F32 = mybir.dt.float32
U32 = mybir.dt.uint32
U8 = mybir.dt.uint8
FP8X4 = mybir.dt.float8_e4m3fn_x4
ALU = mybir.AluOpType

P = 128
B = 16
D = 512
M = 512
C = D // P
FLOPS = 2 * B * D * D * M

INV_M = 1.0 / M
MEAN_N = 32
PE_CHUNKS = (0, 1, 2)


def x_on_vector(b, h):
    return h == 0 and b > 4 and b % 5 == 1


def xi_on_vector(b, h):
    return h == 0 or b < B - 2


def on_gpsimd(b, c):
    return c == 3 and b >= 3


def y_on_vector(b, c):
    return b == B - 1 and c % 2 == 1


def tile_covpool_pa_kernel(tc, x, out):
    nc = tc.nc
    x_rows = x.rearrange("b (p c) h w -> b p (c h w)", c=C)
    out_rows = out.rearrange("b (p c) j -> b p (c j)", c=C)

    with ExitStack() as ctx:
        const = ctx.enter_context(tc.tile_pool(name="const", bufs=1))
        xin = ctx.enter_context(tc.tile_pool(name="xin", bufs=1))
        grp = ctx.enter_context(tc.tile_pool(name="grp", bufs=7))
        cod = ctx.enter_context(tc.tile_pool(name="cod", bufs=3))
        small = ctx.enter_context(tc.tile_pool(name="small", bufs=4))
        junk = ctx.enter_context(tc.tile_pool(name="junk", bufs=2))
        ysb = ctx.enter_context(tc.tile_pool(name="ysb", bufs=4))
        psum = ctx.enter_context(tc.psum_pool(name="psum", bufs=8))
        ctx.enter_context(tc.manual_schedule())

        ident = const.tile([P, P], F32, name="ident")
        masks.make_identity(nc, ident[:])
        warm_t = const.tile([P, P], F32, name="warm_t")
        nc.vector.memset(warm_t[:], 1.0)
        inv_m = const.tile([P, MEAN_N], BF16, name="inv_m")
        nc.vector.memset(inv_m[:], INV_M)

        x_sb = []
        for b in range(B):
            t = xin.tile([P, C * M], BF16, name="x%d" % b)
            pieces = C if b == 0 else 1
            w = C * M // pieces
            for i in range(pieces):
                nc.sync.dma_start(out=t[:, i * w : (i + 1) * w], in_=x_rows[b][:, i * w : (i + 1) * w])
            x_sb.append(t)

        st = [{} for _ in range(B)]

        def copy(on_vector, dst, src):
            if on_vector:
                nc.vector.tensor_copy(out=dst, in_=src)
            else:
                nc.scalar.copy(out=dst, in_=src)

        def transpose_half(src, h, warm=0):
            tp = psum.tile([P, 4, P], F32, name="tp", tag="bank")
            for k in range(warm):
                nc.tensor.matmul(
                    tp[:, 0, :], lhsT=warm_t[:], rhs=warm_t[:], start=True, stop=True
                )
            sw = src[:].bitcast(F32)
            for k in range(4):
                col = (4 * h + k) * P
                nc.tensor.transpose(tp[:, k, :], sw[:, col : col + P], ident[:])
            return tp

        def group_half(on_vector, dst, tp, h):
            copy(
                on_vector,
                dst[:].bitcast(F32)[:, h * 512 : (h + 1) * 512].rearrange("p (c r u) -> p c r u", c=2, u=2),
                tp[:].rearrange("p (c u) r -> p c r u", c=2),
            )

        def quantise(b, src, name):
            codes = cod.tile([P, D], U32, name=name + "c", align_bytes=64)
            scales = cod.tile([P, D], U8, name=name + "s", align_bytes=64)
            nc.vector.quantize_mx(out=codes[:].bitcast(FP8X4), scales=scales[:], in_=st[b][src][:])
            st[b][name] = (codes, scales)

        def qx(b):
            if at(b):
                quantise(b, "x_g", "x_q")

        def qi(b):
            if at(b):
                quantise(b, "xi_g", "xi_q")

        def qi_half(b, h):
            s = st[b]
            if h == 0:
                codes = cod.tile([P, D], U32, name="xi_qc", align_bytes=64)
                scales = cod.tile([P, D], U8, name="xi_qs", align_bytes=64)
                s["xi_q"] = (codes, scales)
            lo, hi = h * D // 2, (h + 1) * D // 2
            nc.vector.quantize_mx(
                out=s["xi_q"][0][:, lo:hi].bitcast(FP8X4),
                scales=s["xi_q"][1][:, lo:hi],
                in_=s["xi_g"][:, 4 * lo : 4 * hi],
            )

        def ta(b, h, warm=0):
            if at(b):
                st[b]["tx", h] = transpose_half(x_sb[b], h, warm)

        def bx(b, h):
            if at(b):
                if "x_g" not in st[b]:
                    st[b]["x_g"] = grp.tile([P, D * 4], BF16, name="x_g", align_bytes=64)
                group_half(x_on_vector(b, h), st[b]["x_g"], st[b]["tx", h], h)

        def sums(b, c):
            if at(b) and (b < 1 or c not in PE_CHUNKS):
                if "mean" not in st[b]:
                    st[b]["mean"] = small.tile([P, C], F32, name="mean")
                factor = -INV_M * INV_M if on_gpsimd(b, c) else INV_M
                jv = junk.tile([P, M], BF16, name="jv")
                nc.vector.tensor_scalar(
                    out=jv[:], in0=x_sb[b][:, c * M : (c + 1) * M], scalar1=factor, scalar2=None,
                    op0=ALU.mult, op1=ALU.add, accum_out=st[b]["mean"][:, c : c + 1],
                )

        def pe_means(b):
            if not at(b) or b < 1:
                return
            ms_bank = psum.tile([P, D], F32, name="ms", tag="bank")
            ms = ms_bank[:, : C * MEAN_N].rearrange("p (c n) -> p c n", c=C)
            xv = st[b]["x_g"][:].rearrange("p (n t) -> p n t", t=4)
            for c in PE_CHUNKS:
                for t in range(4):
                    nc.tensor.matmul(
                        ms[:, c, :],
                        lhsT=xv[:, c * P : (c + 1) * P, t],
                        rhs=inv_m[:],
                        start=(t == 0),
                        stop=(t == 3),
                    )
            st[b]["ms"] = ms

        def centre(b, c):
            if at(b):
                if "xi" not in st[b]:
                    st[b]["xi"] = grp.tile([P, C * M], BF16, name="xi")
                if on_gpsimd(b, c):
                    nc.gpsimd.tensor_scalar(
                        out=st[b]["xi"][:, c * M : (c + 1) * M],
                        in0=x_sb[b][:, c * M : (c + 1) * M],
                        scalar1=INV_M,
                        scalar2=st[b]["mean"][:, c : c + 1],
                        op0=ALU.mult,
                        op1=ALU.add,
                    )
                    return
                if c in PE_CHUNKS and b >= 1:
                    mean = st[b]["ms"][:, c, 0:1]
                else:
                    mean = st[b]["mean"][:, c : c + 1]
                nc.vector.tensor_scalar(
                    out=st[b]["xi"][:, c * M : (c + 1) * M],
                    in0=x_sb[b][:, c * M : (c + 1) * M],
                    scalar1=mean,
                    scalar2=INV_M,
                    op0=ALU.subtract,
                    op1=ALU.mult,
                )

        def tf(b, h, warm=0):
            if at(b):
                st[b]["ti", h] = transpose_half(st[b]["xi"], h, warm)

        def gi(b, h, first=False):
            if at(b):
                if h == 0 and "xi_g" not in st[b] or first:
                    st[b]["xi_g"] = grp.tile([P, D * 4], BF16, name="xi_g", align_bytes=64)
                group_half(xi_on_vector(b, h), st[b]["xi_g"], st[b]["ti", h], h)

        def mx(b, c):
            if not at(b):
                return
            s = st[b]
            y_ps = psum.tile([P, D], F32, name="y_ps", tag="bank")
            nc.tensor.matmul_mx(
                out=y_ps[:],
                lhsT=s["xi_q"][0][:, c * P : (c + 1) * P].bitcast(FP8X4),
                lhsT_scale=s["xi_q"][1][:, c * P : (c + 1) * P],
                rhs=s["x_q"][0][:].bitcast(FP8X4),
                rhs_scale=s["x_q"][1][:],
                start=True,
                stop=True,
            )
            s["yp", c] = y_ps

        def y_out(b, c):
            if not at(b):
                return
            if c == 0:
                st[b]["y"] = ysb.tile([P, C * D], F32, name="y_sb")
            y_sb = st[b]["y"]
            copy(
                y_on_vector(b, c),
                y_sb[:, c * D : (c + 1) * D].rearrange("p (r c) -> p r c", c=C),
                st[b]["yp", c][:].rearrange("p (c r) -> p r c", c=C),
            )
            if b >= B - 2:
                nc.sync.dma_start(out=out_rows[b][:, c * D : (c + 1) * D], in_=y_sb[:, c * D : (c + 1) * D])
            elif b >= B - 8 and c % 2 == 1:
                nc.sync.dma_start(out=out_rows[b][:, (c - 1) * D : (c + 1) * D], in_=y_sb[:, (c - 1) * D : (c + 1) * D])
            elif b < B - 8 and c == C - 1:
                nc.sync.dma_start(out=out_rows[b], in_=y_sb[:])

        def at(b):
            return 0 <= b < B

        ta(0, 0, 7)
        bx(0, 0)
        ta(0, 1)
        bx(0, 1)
        sums(0, 0)
        sums(0, 1)
        centre(0, 0)
        centre(0, 1)
        sums(0, 2)
        sums(0, 3)
        centre(0, 2)
        centre(0, 3)
        ta(1, 0, 2)
        bx(1, 0)
        ta(1, 1)
        bx(1, 1)
        tf(0, 0)
        tf(0, 1)
        sums(1, 3)
        qx(0)
        gi(0, 0)
        gi(0, 1)
        ta(2, 0)
        ta(2, 1)
        pe_means(1)
        bx(2, 0)
        bx(2, 1)
        sums(2, 3)
        ta(3, 0)
        ta(3, 1)
        centre(1, 0)
        centre(1, 1)
        centre(1, 2)
        centre(1, 3)
        pe_means(2)
        bx(3, 0)
        bx(3, 1)
        ta(4, 0)
        ta(4, 1)
        bx(4, 0)
        bx(4, 1)
        for j in range(B):
            qi(j)
            tf(j + 1, 0)
            tf(j + 1, 1)
            centre(j + 2, 0)
            centre(j + 2, 1)
            centre(j + 2, 2)
            if not on_gpsimd(j + 2, 3):
                centre(j + 2, 3)
            if x_on_vector(j + 4, 0):
                bx(j + 4, 0)
            mx(j, 0)
            mx(j, 1)
            mx(j, 2)
            mx(j, 3)
            pe_means(j + 3)
            sums(j + 3, 3)
            if on_gpsimd(j + 3, 3):
                centre(j + 3, 3)
            gi(j + 1, 0)
            gi(j + 1, 1)
            qx(j + 1)
            y_out(j, 0)
            y_out(j, 1)
            y_out(j, 2)
            y_out(j, 3)
            ta(j + 5, 0)
            ta(j + 5, 1)
            if not x_on_vector(j + 5, 0):
                bx(j + 5, 0)
            bx(j + 5, 1)
